import numpy as np
import ml_dtypes


def mxq(x, axis, fmt="e4m3"):
    dtype, down = {"e4m3": (ml_dtypes.float8_e4m3fn, 7), "e5m2": (ml_dtypes.float8_e5m2, 14)}[fmt]
    v = np.moveaxis(np.asarray(x, np.float32).astype(ml_dtypes.bfloat16).astype(np.float64), axis, -1)
    blocks = v.reshape(v.shape[:-1] + (-1, 32))
    amax = np.abs(blocks).max(-1, keepdims=True)
    byte = np.maximum(np.where(amax > 0, np.frexp(amax)[1] - 1 + 127, 0) - down, 1)
    scale = np.exp2(byte - 127.0)
    codes = (blocks / scale).astype(np.float32).astype(dtype).astype(np.float64)
    return np.moveaxis((codes * scale).reshape(v.shape), -1, axis)


WIDE = False


def mx_kscale(k):
    if not WIDE:
        return np.ones(k)
    levels = np.array([10, -10, 5, -5, 0])
    a = np.random.permutation(np.resize(levels, k // 512 * 4)).reshape(k // 512, 4)
    idx = np.arange(k)
    return np.exp2(a[idx // 512, idx % 128 // 32])


BF16 = ml_dtypes.bfloat16


def bf(x):
    return np.asarray(x, np.float32).astype(BF16)


def f64(x):
    return np.asarray(x).astype(np.float64)


C, W, H = 512, 64, 32
N = W * H


def setup_inputs():
    g = np.random.standard_normal((C, 1))
    u = np.random.standard_normal((1, N))
    r = mx_kscale(N)
    return {"x": bf(((np.random.standard_normal((C, N)) + g * u) * r[None, :]).reshape(C, W, H))}


def reference(x):
    q = f64(x).reshape(C, N).T
    q_norm = np.sqrt((q * q).sum(axis=1))
    qq = mxq(q, 1, "e4m3")
    energy = qq @ qq.T
    nm = q_norm[:, None] * q_norm[None, :]
    norm_energy = energy / nm
    e = np.exp(norm_energy - norm_energy.max(axis=-1, keepdims=True))
    attention = e / e.sum(axis=-1, keepdims=True)
    return attention[None]

@@ -1,0 +1,256 @@
+from contextlib import ExitStack
+
+import concourse.mybir as mybir
+from concourse.masks import make_identity
+
+F32 = mybir.dt.float32
+BF16 = mybir.dt.bfloat16
+U32 = mybir.dt.uint32
+U8 = mybir.dt.uint8
+FP8X4 = mybir.dt.float8_e4m3fn_x4
+ACT = mybir.ActivationFunctionType
+ALU = mybir.AluOpType
+AX = mybir.AxisListType
+
+P = 128
+C = 512
+N = 2048
+PACK = 4
+CHUNK = 512
+NCH = N // CHUNK
+NT = N // P
+BPC = CHUNK // P
+FLOPS = 2 * N * N * C
+VSHARE = 320
+
+
+def tile_cos_attn_kernel(tc, x, out):
+    nc = tc.nc
+    xv = x.rearrange("(p j) w h -> p j (w h)", j=PACK)
+    ov = out.rearrange("o (t p) n -> (o t) p n", p=P)
+    with ExitStack() as ctx:
+        ctx.enter_context(tc.manual_schedule())
+        const = ctx.enter_context(tc.tile_pool(name="const", bufs=1))
+        rows = ctx.enter_context(tc.tile_pool(name="rows", bufs=8))
+        psum = ctx.enter_context(tc.psum_pool(name="psum", bufs=8))
+
+        raw = []
+        for c in range(NCH):
+            r = const.tile([P, PACK, CHUNK], BF16, name="raw%d" % c)
+            nc.sync.dma_start(out=r[:], in_=xv[:, :, c * CHUNK:(c + 1) * CHUNK])
+            raw.append(r)
+
+        ident = const.tile([P, P], F32, name="ident")
+        make_identity(nc, ident[:])
+        ones = const.tile([P, 2], F32, name="ones")
+        nc.vector.memset(ones[:], 1.0)
+        warm = const.tile([P, 2], F32, name="warm")
+        nc.scalar.activation(out=warm[:, 0:1], in_=ones[:, 0:1], func=ACT.Abs_reciprocal_sqrt)
+
+        codes = const.tile([P, N], U32, name="codes", align_bytes=64)
+        scl = const.tile([P, N], U8, name="scl", align_bytes=64)
+        rnj = const.tile([P, N], F32, name="rnj")
+        rn = const.tile([P, NT], F32, name="rn")
+        ssum = const.tile([P, NT], F32, name="ssum")
+        s0p = const.tile([P, NCH], F32, name="s0p")
+        s0 = const.tile([P, 1], F32, name="s0")
+        rs = const.tile([P, NT], F32, name="rs")
+        grouped = [const.tile([P, CHUNK, PACK], BF16, name="grouped%d" % c, align_bytes=64) for c in range(NCH)]
+        dd = [const.tile([P, CHUNK], F32, name="dd%d" % c) for c in range(NCH)]
+        n2 = psum.tile([P, CHUNK], F32, name="n2", tag="b")
+        gg = {}
+        bb = {}
+        pp = {}
+        rr = {}
+
+        def cols(c):
+            return slice(c * CHUNK, (c + 1) * CHUNK)
+
+        def tcols(c):
+            return slice(c * BPC, (c + 1) * BPC)
+
+        def regroup_v(c):
+            dst = grouped[c][:].rearrange("p (c i) t -> p c t i", i=4)
+            src = raw[c][:].rearrange("p t (c i) -> p c t i", i=4)
+            k = VSHARE // 4
+            nc.vector.tensor_copy(out=dst[:, :k], in_=src[:, :k])
+
+        def regroup_s(c):
+            dst = grouped[c][:].rearrange("p (c i) t -> p c t i", i=4)
+            src = raw[c][:].rearrange("p t (c i) -> p c t i", i=4)
+            k = VSHARE // 4
+            nc.scalar.copy(out=dst[:, k:], in_=src[:, k:])
+
+        def gram(c):
+            g = psum.tile([P, CHUNK], F32, name="g", tag="b")
+            gg[c] = g
+            for b in range(BPC):
+                bs = slice(b * P, (b + 1) * P)
+                for j in range(PACK):
+                    nc.tensor.matmul(
+                        out=g[:, bs], lhsT=raw[c][:, j, bs], rhs=raw[c][:, j, bs],
+                        start=(j == 0), stop=(j == PACK - 1),
+                    )
+
+        def mask(c):
+            nc.vector.tensor_tensor(
+                out=dd[c][:].rearrange("p (b n) -> p b n", b=BPC),
+                in0=gg[c][:].rearrange("p (b n) -> p b n", b=BPC),
+                in1=ident[:].unsqueeze(1).to_broadcast([P, BPC, P]),
+                op=ALU.mult,
+            )
+
+        def n2mm(c):
+            for b in range(BPC):
+                t = c * BPC + b
+                nc.tensor.matmul(
+                    out=n2[:, t:t + 1], lhsT=dd[c][:, b * P:(b + 1) * P], rhs=ones[:, 0:1],
+                    start=True, stop=True,
+                )
+
+        def rsq_s(c):
+            nc.scalar.activation(out=rn[:, tcols(c)], in_=n2[:, tcols(c)], func=ACT.Abs_reciprocal_sqrt)
+
+        def rsq_v(c):
+            return
+
+        def spread(c):
+            bc = psum.tile([P, CHUNK], F32, name="bc", tag="b")
+            bb[c] = bc
+            for b in range(BPC):
+                t = c * BPC + b
+                nc.tensor.transpose(
+                    out=bc[:, b * P:(b + 1) * P],
+                    in_=rn[:, t:t + 1].to_broadcast([P, P]),
+                    identity=ident[:],
+                )
+
+        def quant(c):
+            nc.vector.quantize_mx(
+                out=codes[:, cols(c)].bitcast(FP8X4),
+                scales=scl[:, cols(c)],
+                in_=grouped[c][:].rearrange("p w t -> p (w t)"),
+            )
+
+        def mx(i, c):
+            ms = slice(i * P, (i + 1) * P)
+            ps = psum.tile([P, CHUNK], F32, name="ps", tag="b")
+            pp[(i, c)] = ps
+            nc.tensor.matmul_mx(
+                out=ps[:],
+                lhsT=codes[:, ms].bitcast(FP8X4), lhsT_scale=scl[:, ms],
+                rhs=codes[:, cols(c)].bitcast(FP8X4), rhs_scale=scl[:, cols(c)],
+                start=True, stop=True,
+            )
+
+        def scale(i, c):
+            if c == 0:
+                rr[i] = rows.tile([P, N], F32, name="row")
+            nc.vector.scalar_tensor_tensor(
+                out=rr[i][:, cols(c)], in0=pp[(i, c)][:], scalar=rn[:, i:i + 1], in1=rnj[:, cols(c)],
+                op0=ALU.mult, op1=ALU.mult,
+            )
+
+        def expo(i, sl, acc):
+            bias = -1.0
+            nc.scalar.activation(
+                out=rr[i][:, sl], in_=rr[i][:, sl], func=ACT.Exp, bias=bias, scale=1.0,
+                accum_out=acc,
+            )
+
+        def finish(i):
+            r1 = rs[:, i:i + 1]
+            row = rr[i]
+            if i == 0:
+                nc.vector.tensor_reduce(out=s0[:], in_=s0p[:], axis=AX.X, op=ALU.add)
+                nc.vector.reciprocal(out=r1, in_=s0[:])
+            else:
+                nc.vector.reciprocal(out=r1, in_=ssum[:, i:i + 1])
+            if i < NT - 2:
+                nc.gpsimd.tensor_scalar(
+                    out=row[:], in0=row[:], scalar1=r1, scalar2=1.0, op0=ALU.mult, op1=ALU.mult,
+                )
+                nc.sync.dma_start(out=ov[i], in_=row[:])
+            elif i == NT - 2:
+                for h in range(2):
+                    sl = slice(h * 1024, (h + 1) * 1024)
+                    nc.vector.tensor_scalar(out=row[:, sl], in0=row[:, sl], scalar1=r1, scalar2=None, op0=ALU.mult)
+                    nc.sync.dma_start(out=ov[i][:, sl], in_=row[:, sl])
+            else:
+                a = slice(0, 1024)
+                b = slice(1024, 1536)
+                d = slice(1536, 2048)
+                nc.gpsimd.tensor_scalar(
+                    out=row[:, d], in0=row[:, d], scalar1=r1, scalar2=1.0, op0=ALU.mult, op1=ALU.mult,
+                )
+                nc.scalar.activation(out=row[:, b], in_=row[:, b], func=ACT.Copy, scale=r1)
+                nc.vector.tensor_scalar(out=row[:, a], in0=row[:, a], scalar1=r1, scalar2=None, op0=ALU.mult)
+                nc.sync.dma_start(out=ov[i][:, a], in_=row[:, a])
+                nc.sync.dma_start(out=ov[i][:, b], in_=row[:, b])
+                nc.sync.dma_start(out=ov[i][:, d], in_=row[:, d])
+
+        def copy_s(c):
+            nc.scalar.copy(out=rnj[:, cols(c)], in_=bb[c][:])
+
+        regroup_v(0)
+        regroup_s(0)
+        gram(0)
+        mask(0)
+        regroup_v(1)
+        regroup_s(1)
+        gram(1)
+        n2mm(0)
+        rsq_s(0)
+        quant(0)
+        mask(1)
+        regroup_v(2)
+        regroup_s(2)
+        gram(2)
+        n2mm(1)
+        rsq_s(1)
+        quant(1)
+        mask(2)
+        gram(3)
+        regroup_s(3)
+        rsq_v(0)
+        spread(0)
+        copy_s(0)
+        n2mm(2)
+        rsq_s(2)
+        mask(3)
+        rsq_v(1)
+        spread(1)
+        copy_s(1)
+        n2mm(3)
+        rsq_s(3)
+        regroup_v(3)
+        rsq_v(2)
+        spread(2)
+        copy_s(2)
+        quant(2)
+        quant(3)
+        rsq_v(3)
+        mx(0, 0)
+        mx(0, 1)
+        mx(0, 2)
+        spread(3)
+        nc.scalar.activation(out=warm[:, 1:2], in_=ones[:, 0:1], func=ACT.Exp)
+        mx(0, 3)
+
+        when = {(1, 1): 0, (2, 2): 1}
+        for i in range(2, NT):
+            when[(i + 2, 0)] = i
+        for i in range(NT + 2):
+            for c in range(NCH):
+                if i < NT:
+                    if i > 0:
+                        mx(i, c)
+                    if i == 0 and c == 3:
+                        nc.vector.tensor_copy(out=rnj[:, cols(3)], in_=bb[3][:])
+                    scale(i, c)
+                    if i == 0:
+                        expo(0, cols(c), s0p[:, c:c + 1])
+                if (i, c) in when:
+                    finish(when[(i, c)])
+            if 0 < i < NT:
+                expo(i, slice(0, N), ssum[:, i:i + 1])

@@ -21,7 +21,9 @@ NCH = N // CHUNK
 NT = N // P
 BPC = CHUNK // P
 FLOPS = 2 * N * N * C
-VSHARE = 320
+CH = [(0,256),(256,256),(512,512),(1024,512),(1536,512)]
+NK = len(CH)
+NWARM = 4
 
 
 def tile_cos_attn_kernel(tc, x, out):
@@ -35,11 +37,18 @@ def tile_cos_attn_kernel(tc, x, out):
         psum = ctx.enter_context(tc.psum_pool(name="psum", bufs=8))
 
         raw = []
-        for c in range(NCH):
-            r = const.tile([P, PACK, CHUNK], BF16, name="raw%d" % c)
-            nc.sync.dma_start(out=r[:], in_=xv[:, :, c * CHUNK:(c + 1) * CHUNK])
+        for k in range(NK):
+            st, sz = CH[k]
+            r = const.tile([P, PACK, sz], BF16, name="raw%d" % k)
+            nc.sync.dma_start(out=r[:], in_=xv[:, :, st:st + sz])
             raw.append(r)
 
+        if NWARM:
+            wz = const.tile([P, CHUNK], BF16, name="wz")
+            nc.vector.memset(wz[:], 0.0)
+            wp = psum.tile([P, CHUNK], F32, name="wp", tag="b")
+            for w in range(NWARM):
+                nc.tensor.matmul(out=wp[:], lhsT=wz[:, 0:P], rhs=wz[:], start=True, stop=True)
         ident = const.tile([P, P], F32, name="ident")
         make_identity(nc, ident[:])
         ones = const.tile([P, 2], F32, name="ones")
@@ -55,8 +64,8 @@ def tile_cos_attn_kernel(tc, x, out):
         s0p = const.tile([P, NCH], F32, name="s0p")
         s0 = const.tile([P, 1], F32, name="s0")
         rs = const.tile([P, NT], F32, name="rs")
-        grouped = [const.tile([P, CHUNK, PACK], BF16, name="grouped%d" % c, align_bytes=64) for c in range(NCH)]
-        dd = [const.tile([P, CHUNK], F32, name="dd%d" % c) for c in range(NCH)]
+        grouped = [const.tile([P, CH[k][1], PACK], BF16, name="grouped%d" % k, align_bytes=64) for k in range(NK)]
+        dd = [const.tile([P, CH[k][1]], F32, name="dd%d" % k) for k in range(NK)]
         n2 = psum.tile([P, CHUNK], F32, name="n2", tag="b")
         gg = {}
         bb = {}
@@ -66,70 +75,78 @@ def tile_cos_attn_kernel(tc, x, out):
         def cols(c):
             return slice(c * CHUNK, (c + 1) * CHUNK)
 
-        def tcols(c):
-            return slice(c * BPC, (c + 1) * BPC)
+        def kcols(k):
+            return slice(CH[k][0], CH[k][0] + CH[k][1])
 
-        def regroup_v(c):
-            dst = grouped[c][:].rearrange("p (c i) t -> p c t i", i=4)
-            src = raw[c][:].rearrange("p t (c i) -> p c t i", i=4)
-            k = VSHARE // 4
-            nc.vector.tensor_copy(out=dst[:, :k], in_=src[:, :k])
+        def tcols(k):
+            return slice(CH[k][0] // P, (CH[k][0] + CH[k][1]) // P)
 
-        def regroup_s(c):
-            dst = grouped[c][:].rearrange("p (c i) t -> p c t i", i=4)
-            src = raw[c][:].rearrange("p t (c i) -> p c t i", i=4)
-            k = VSHARE // 4
-            nc.scalar.copy(out=dst[:, k:], in_=src[:, k:])
+        def vshare(k):
+            return (CH[k][1] * 5 // 8) // 8 * 2
 
-        def gram(c):
+        def regroup_v(k):
+            dst = grouped[k][:].rearrange("p (c i) t -> p c t i", i=4)
+            src = raw[k][:].rearrange("p t (c i) -> p c t i", i=4)
+            nc.vector.tensor_copy(out=dst[:, :vshare(k)], in_=src[:, :vshare(k)])
+
+        def regroup_s(k):
+            dst = grouped[k][:].rearrange("p (c i) t -> p c t i", i=4)
+            src = raw[k][:].rearrange("p t (c i) -> p c t i", i=4)
+            nc.scalar.copy(out=dst[:, vshare(k):], in_=src[:, vshare(k):])
+
+        def gram(k):
             g = psum.tile([P, CHUNK], F32, name="g", tag="b")
-            gg[c] = g
-            for b in range(BPC):
+            gg[k] = g
+            for b in range(CH[k][1] // P):
                 bs = slice(b * P, (b + 1) * P)
                 for j in range(PACK):
                     nc.tensor.matmul(
-                        out=g[:, bs], lhsT=raw[c][:, j, bs], rhs=raw[c][:, j, bs],
+                        out=g[:, bs], lhsT=raw[k][:, j, bs], rhs=raw[k][:, j, bs],
                         start=(j == 0), stop=(j == PACK - 1),
                     )
 
-        def mask(c):
+        def mask(k):
+            nb = CH[k][1] // P
             nc.vector.tensor_tensor(
-                out=dd[c][:].rearrange("p (b n) -> p b n", b=BPC),
-                in0=gg[c][:].rearrange("p (b n) -> p b n", b=BPC),
-                in1=ident[:].unsqueeze(1).to_broadcast([P, BPC, P]),
+                out=dd[k][:].rearrange("p (b n) -> p b n", b=nb),
+                in0=gg[k][:, 0:CH[k][1]].rearrange("p (b n) -> p b n", b=nb),
+                in1=ident[:].unsqueeze(1).to_broadcast([P, nb, P]),
                 op=ALU.mult,
             )
 
-        def n2mm(c):
-            for b in range(BPC):
-                t = c * BPC + b
+        def n2mm(k):
+            for b in range(CH[k][1] // P):
+                t = CH[k][0] // P + b
                 nc.tensor.matmul(
-                    out=n2[:, t:t + 1], lhsT=dd[c][:, b * P:(b + 1) * P], rhs=ones[:, 0:1],
+                    out=n2[:, t:t + 1], lhsT=dd[k][:, b * P:(b + 1) * P], rhs=ones[:, 0:1],
                     start=True, stop=True,
                 )
 
-        def rsq_s(c):
-            nc.scalar.activation(out=rn[:, tcols(c)], in_=n2[:, tcols(c)], func=ACT.Abs_reciprocal_sqrt)
+        def rsq(k):
+            nc.scalar.activation(out=rn[:, tcols(k)], in_=n2[:, tcols(k)], func=ACT.Abs_reciprocal_sqrt)
 
-        def rsq_v(c):
-            return
-
-        def spread(c):
+        def spread(k):
             bc = psum.tile([P, CHUNK], F32, name="bc", tag="b")
-            bb[c] = bc
-            for b in range(BPC):
-                t = c * BPC + b
+            bb[k] = bc
+            for b in range(CH[k][1] // P):
+                t = CH[k][0] // P + b
                 nc.tensor.transpose(
                     out=bc[:, b * P:(b + 1) * P],
                     in_=rn[:, t:t + 1].to_broadcast([P, P]),
                     identity=ident[:],
                 )
 
-        def quant(c):
+        def copy_s(k):
+            nc.scalar.copy(out=rnj[:, kcols(k)], in_=bb[k][:, 0:CH[k][1]])
+
+        def copy_v(k):
+            nc.vector.tensor_copy(out=rnj[:, kcols(k)], in_=bb[k][:, 0:CH[k][1]])
+
+        def quant(k):
             nc.vector.quantize_mx(
-                out=codes[:, cols(c)].bitcast(FP8X4),
-                scales=scl[:, cols(c)],
-                in_=grouped[c][:].rearrange("p w t -> p (w t)"),
+                out=codes[:, kcols(k)].bitcast(FP8X4),
+                scales=scl[:, kcols(k)],
+                in_=grouped[k][:].rearrange("p w t -> p (w t)"),
             )
 
         def mx(i, c):
@@ -152,9 +169,8 @@ def tile_cos_attn_kernel(tc, x, out):
             )
 
         def expo(i, sl, acc):
-            bias = -1.0
             nc.scalar.activation(
-                out=rr[i][:, sl], in_=rr[i][:, sl], func=ACT.Exp, bias=bias, scale=1.0,
+                out=rr[i][:, sl], in_=rr[i][:, sl], func=ACT.Exp, bias=-1.0, scale=1.0,
                 accum_out=acc,
             )
 
@@ -189,51 +205,39 @@ def tile_cos_attn_kernel(tc, x, out):
                 nc.sync.dma_start(out=ov[i][:, b], in_=row[:, b])
                 nc.sync.dma_start(out=ov[i][:, d], in_=row[:, d])
 
-        def copy_s(c):
-            nc.scalar.copy(out=rnj[:, cols(c)], in_=bb[c][:])
-
-        regroup_v(0)
-        regroup_s(0)
-        gram(0)
-        mask(0)
-        regroup_v(1)
-        regroup_s(1)
-        gram(1)
-        n2mm(0)
-        rsq_s(0)
-        quant(0)
-        mask(1)
-        regroup_v(2)
-        regroup_s(2)
-        gram(2)
-        n2mm(1)
-        rsq_s(1)
-        quant(1)
-        mask(2)
-        gram(3)
-        regroup_s(3)
-        rsq_v(0)
-        spread(0)
-        copy_s(0)
-        n2mm(2)
-        rsq_s(2)
-        mask(3)
-        rsq_v(1)
-        spread(1)
-        copy_s(1)
-        n2mm(3)
-        rsq_s(3)
-        regroup_v(3)
-        rsq_v(2)
-        spread(2)
-        copy_s(2)
-        quant(2)
-        quant(3)
-        rsq_v(3)
+        last = NK - 1
+        for k in range(last):
+            regroup_v(k)
+            regroup_s(k)
+            gram(k)
+            if k >= 3:
+                spread(k - 3)
+                copy_s(k - 3)
+            if k >= 1:
+                n2mm(k - 1)
+                rsq(k - 1)
+                quant(k - 1)
+            mask(k)
+        gram(last)
+        regroup_s(last)
+        spread(last - 3)
+        copy_s(last - 3)
+        n2mm(last - 1)
+        rsq(last - 1)
+        mask(last)
+        spread(last - 2)
+        copy_s(last - 2)
+        n2mm(last)
+        rsq(last)
+        regroup_v(last)
+        spread(last - 1)
+        copy_s(last - 1)
+        quant(last - 1)
+        quant(last)
         mx(0, 0)
         mx(0, 1)
         mx(0, 2)
-        spread(3)
+        spread(last)
         nc.scalar.activation(out=warm[:, 1:2], in_=ones[:, 0:1], func=ACT.Exp)
         mx(0, 3)
 
@@ -246,7 +250,7 @@ def tile_cos_attn_kernel(tc, x, out):
                     if i > 0:
                         mx(i, c)
                     if i == 0 and c == 3:
-                        nc.vector.tensor_copy(out=rnj[:, cols(3)], in_=bb[3][:])
+                        copy_v(last)
                     scale(i, c)
                     if i == 0:
                         expo(0, cols(c), s0p[:, c:c + 1])

@@ -23,7 +23,9 @@ BPC = CHUNK // P
 FLOPS = 2 * N * N * C
 CH = [(0,256),(256,256),(512,512),(1024,512),(1536,512)]
 NK = len(CH)
-NWARM = 4
+NWARM = 3
+MIR = [0,0,0,0,1,1,1,1,2,2,2,2,2,2,2,2]
+NSRC = 8
 
 
 def tile_cos_attn_kernel(tc, x, out):
@@ -53,6 +55,8 @@ def tile_cos_attn_kernel(tc, x, out):
         make_identity(nc, ident[:])
         ones = const.tile([P, 2], F32, name="ones")
         nc.vector.memset(ones[:], 1.0)
+        sall = const.tile([P, NT, 16], F32, name="sall")
+        nc.vector.memset(sall[:], 0.0)
         warm = const.tile([P, 2], F32, name="warm")
         nc.scalar.activation(out=warm[:, 0:1], in_=ones[:, 0:1], func=ACT.Abs_reciprocal_sqrt)
 
@@ -60,17 +64,17 @@ def tile_cos_attn_kernel(tc, x, out):
         scl = const.tile([P, N], U8, name="scl", align_bytes=64)
         rnj = const.tile([P, N], F32, name="rnj")
         rn = const.tile([P, NT], F32, name="rn")
-        ssum = const.tile([P, NT], F32, name="ssum")
-        s0p = const.tile([P, NCH], F32, name="s0p")
-        s0 = const.tile([P, 1], F32, name="s0")
+        stot = const.tile([P, NT], F32, name="stot")
         rs = const.tile([P, NT], F32, name="rs")
         grouped = [const.tile([P, CH[k][1], PACK], BF16, name="grouped%d" % k, align_bytes=64) for k in range(NK)]
         dd = [const.tile([P, CH[k][1]], F32, name="dd%d" % k) for k in range(NK)]
+        keep = [const.tile([P, N], F32, name="keep%d" % i) for i in range(NSRC)]
         n2 = psum.tile([P, CHUNK], F32, name="n2", tag="b")
         gg = {}
         bb = {}
         pp = {}
-        rr = {}
+        tt = {}
+        ee = {}
 
         def cols(c):
             return slice(c * CHUNK, (c + 1) * CHUNK)
@@ -149,6 +153,14 @@ def tile_cos_attn_kernel(tc, x, out):
                 in_=grouped[k][:].rearrange("p w t -> p (w t)"),
             )
 
+        def etile(i):
+            if i not in ee:
+                if i < NSRC:
+                    ee[i] = keep[i]
+                else:
+                    ee[i] = rows.tile([P, N], F32, name="row")
+            return ee[i]
+
         def mx(i, c):
             ms = slice(i * P, (i + 1) * P)
             ps = psum.tile([P, CHUNK], F32, name="ps", tag="b")
@@ -161,49 +173,72 @@ def tile_cos_attn_kernel(tc, x, out):
             )
 
         def scale(i, c):
-            if c == 0:
-                rr[i] = rows.tile([P, N], F32, name="row")
             nc.vector.scalar_tensor_tensor(
-                out=rr[i][:, cols(c)], in0=pp[(i, c)][:], scalar=rn[:, i:i + 1], in1=rnj[:, cols(c)],
+                out=etile(i)[:, cols(c)], in0=pp[(i, c)][:], scalar=rn[:, i:i + 1], in1=rnj[:, cols(c)],
                 op0=ALU.mult, op1=ALU.mult,
             )
 
-        def expo(i, sl, acc):
+        def expo(i, sl, slot):
+            e = etile(i)
             nc.scalar.activation(
-                out=rr[i][:, sl], in_=rr[i][:, sl], func=ACT.Exp, bias=-1.0, scale=1.0,
-                accum_out=acc,
+                out=e[:, sl], in_=e[:, sl], func=ACT.Exp, bias=-1.0, scale=1.0,
+                accum_out=sall[:, i, slot:slot + 1],
             )
+
+        def mirror(i, c):
+            for on_v, a, b in pieces(i, c):
+                t = psum.tile([P, CHUNK], F32, name="tr", tag="b")
+                tt[(i, c, on_v)] = t
+                for blk in range(a // P, b // P):
+                    nc.tensor.transpose(
+                        out=t[:, blk * P:(blk + 1) * P],
+                        in_=keep[c * BPC + blk][:, i * P:(i + 1) * P],
+                        identity=ident[:],
+                    )
+
+        def pieces(i, c):
+            if MIR[i] == 1:
+                if i % 2 == 0:
+                    return [(False, 0, CHUNK)]
+                return [(True, 0, CHUNK // 2), (False, CHUNK // 2, CHUNK)]
+            return [(c == 0, 0, CHUNK)]
+
+        def leave(i, c, vector):
+            e = etile(i)
+            for on_v, a, b in pieces(i, c):
+                if on_v != vector:
+                    continue
+                dst = e[:, c * CHUNK + a:c * CHUNK + b]
+                if on_v:
+                    nc.vector.tensor_scalar(
+                        out=dst, in0=tt[(i, c, on_v)][:, a:b], scalar1=1.0, scalar2=None,
+                        op0=ALU.mult, op1=ALU.add, accum_out=sall[:, i, 8 + c:9 + c],
+                    )
+                else:
+                    nc.scalar.activation(
+                        out=dst, in_=tt[(i, c, on_v)][:, a:b], func=ACT.Copy,
+                        accum_out=sall[:, i, 4 + c:5 + c],
+                    )
 
         def finish(i):
             r1 = rs[:, i:i + 1]
-            row = rr[i]
-            if i == 0:
-                nc.vector.tensor_reduce(out=s0[:], in_=s0p[:], axis=AX.X, op=ALU.add)
-                nc.vector.reciprocal(out=r1, in_=s0[:])
+            e = etile(i)
+            if 0 < i and MIR[i] == 0:
+                nc.vector.reciprocal(out=r1, in_=sall[:, i, 0:1])
             else:
-                nc.vector.reciprocal(out=r1, in_=ssum[:, i:i + 1])
-            if i < NT - 2:
-                nc.gpsimd.tensor_scalar(
-                    out=row[:], in0=row[:], scalar1=r1, scalar2=1.0, op0=ALU.mult, op1=ALU.mult,
-                )
-                nc.sync.dma_start(out=ov[i], in_=row[:])
-            elif i == NT - 2:
-                for h in range(2):
-                    sl = slice(h * 1024, (h + 1) * 1024)
-                    nc.vector.tensor_scalar(out=row[:, sl], in0=row[:, sl], scalar1=r1, scalar2=None, op0=ALU.mult)
-                    nc.sync.dma_start(out=ov[i][:, sl], in_=row[:, sl])
+                nc.vector.tensor_reduce(out=stot[:, i:i + 1], in_=sall[:, i, :], axis=AX.X, op=ALU.add)
+                nc.vector.reciprocal(out=r1, in_=stot[:, i:i + 1])
+            if i < NSRC:
+                o = rows.tile([P, N], F32, name="row")
             else:
-                a = slice(0, 1024)
-                b = slice(1024, 1536)
-                d = slice(1536, 2048)
-                nc.gpsimd.tensor_scalar(
-                    out=row[:, d], in0=row[:, d], scalar1=r1, scalar2=1.0, op0=ALU.mult, op1=ALU.mult,
-                )
-                nc.scalar.activation(out=row[:, b], in_=row[:, b], func=ACT.Copy, scale=r1)
-                nc.vector.tensor_scalar(out=row[:, a], in0=row[:, a], scalar1=r1, scalar2=None, op0=ALU.mult)
-                nc.sync.dma_start(out=ov[i][:, a], in_=row[:, a])
-                nc.sync.dma_start(out=ov[i][:, b], in_=row[:, b])
-                nc.sync.dma_start(out=ov[i][:, d], in_=row[:, d])
+                o = e
+            vcols = (0, 512 * (1 - i % 2), 256)[MIR[i]]
+            nc.gpsimd.tensor_scalar(
+                out=o[:, vcols:], in0=e[:, vcols:], scalar1=r1, scalar2=1.0, op0=ALU.mult, op1=ALU.mult,
+            )
+            if vcols:
+                nc.vector.tensor_scalar(out=o[:, :vcols], in0=e[:, :vcols], scalar1=r1, scalar2=None, op0=ALU.mult)
+            nc.sync.dma_start(out=ov[i], in_=o[:])
 
         last = NK - 1
         for k in range(last):
@@ -241,20 +276,33 @@ def tile_cos_attn_kernel(tc, x, out):
         nc.scalar.activation(out=warm[:, 1:2], in_=ones[:, 0:1], func=ACT.Exp)
         mx(0, 3)
 
-        when = {(1, 1): 0, (2, 2): 1}
-        for i in range(2, NT):
-            when[(i + 2, 0)] = i
-        for i in range(NT + 2):
-            for c in range(NCH):
-                if i < NT:
-                    if i > 0:
-                        mx(i, c)
-                    if i == 0 and c == 3:
+        for k in range(NT + 3):
+            if k + 1 < NT:
+                for c in range(MIR[k + 1], NCH):
+                    mx(k + 1, c)
+            if k < NT:
+                for c in range(MIR[k]):
+                    mirror(k, c)
+            direct = list(range(MIR[k], NCH)) if k < NT else [NCH]
+            for c in direct:
+                if k < NT:
+                    if k == 0 and c == 3:
                         copy_v(last)
-                    scale(i, c)
-                    if i == 0:
-                        expo(0, cols(c), s0p[:, c:c + 1])
-                if (i, c) in when:
-                    finish(when[(i, c)])
-            if 0 < i < NT:
-                expo(i, slice(0, N), ssum[:, i:i + 1])
+                    scale(k, c)
+                    if k == 0:
+                        expo(0, cols(c), c)
+                if c == direct[0]:
+                    if 1 <= k <= NT:
+                        for c2 in range(MIR[k - 1]):
+                            leave(k - 1, c2, True)
+                    if 4 <= k and k - 2 < NT:
+                        finish(k - 2)
+                if k == 1 and c == 1:
+                    finish(0)
+                if k == 2 and c == 2:
+                    finish(1)
+            if 0 < k < NT:
+                expo(k, slice(MIR[k] * CHUNK, N), 0)
+            if k < NT:
+                for c2 in range(MIR[k]):
+                    leave(k, c2, False)

@@ -23,9 +23,7 @@ BPC = CHUNK // P
 FLOPS = 2 * N * N * C
 CH = [(0,256),(256,256),(512,512),(1024,512),(1536,512)]
 NK = len(CH)
-NWARM = 3
-MIR = [0,0,0,0,1,1,1,1,2,2,2,2,2,2,2,2]
-NSRC = 8
+NWARM = 4
 
 
 def tile_cos_attn_kernel(tc, x, out):
@@ -45,18 +43,15 @@ def tile_cos_attn_kernel(tc, x, out):
             nc.sync.dma_start(out=r[:], in_=xv[:, :, st:st + sz])
             raw.append(r)
 
-        if NWARM:
-            wz = const.tile([P, CHUNK], BF16, name="wz")
-            nc.vector.memset(wz[:], 0.0)
-            wp = psum.tile([P, CHUNK], F32, name="wp", tag="b")
-            for w in range(NWARM):
-                nc.tensor.matmul(out=wp[:], lhsT=wz[:, 0:P], rhs=wz[:], start=True, stop=True)
+        wz = const.tile([P, CHUNK], BF16, name="wz")
+        nc.vector.memset(wz[:], 0.0)
+        wp = psum.tile([P, CHUNK], F32, name="wp", tag="b")
+        for w in range(NWARM):
+            nc.tensor.matmul(out=wp[:], lhsT=wz[:, 0:P], rhs=wz[:], start=True, stop=True)
         ident = const.tile([P, P], F32, name="ident")
         make_identity(nc, ident[:])
         ones = const.tile([P, 2], F32, name="ones")
         nc.vector.memset(ones[:], 1.0)
-        sall = const.tile([P, NT, 16], F32, name="sall")
-        nc.vector.memset(sall[:], 0.0)
         warm = const.tile([P, 2], F32, name="warm")
         nc.scalar.activation(out=warm[:, 0:1], in_=ones[:, 0:1], func=ACT.Abs_reciprocal_sqrt)
 
@@ -64,17 +59,15 @@ def tile_cos_attn_kernel(tc, x, out):
         scl = const.tile([P, N], U8, name="scl", align_bytes=64)
         rnj = const.tile([P, N], F32, name="rnj")
         rn = const.tile([P, NT], F32, name="rn")
-        stot = const.tile([P, NT], F32, name="stot")
+        ssum = const.tile([P, NT], F32, name="ssum")
         rs = const.tile([P, NT], F32, name="rs")
         grouped = [const.tile([P, CH[k][1], PACK], BF16, name="grouped%d" % k, align_bytes=64) for k in range(NK)]
         dd = [const.tile([P, CH[k][1]], F32, name="dd%d" % k) for k in range(NK)]
-        keep = [const.tile([P, N], F32, name="keep%d" % i) for i in range(NSRC)]
         n2 = psum.tile([P, CHUNK], F32, name="n2", tag="b")
         gg = {}
         bb = {}
         pp = {}
-        tt = {}
-        ee = {}
+        rr = {}
 
         def cols(c):
             return slice(c * CHUNK, (c + 1) * CHUNK)
@@ -86,7 +79,7 @@ def tile_cos_attn_kernel(tc, x, out):
             return slice(CH[k][0] // P, (CH[k][0] + CH[k][1]) // P)
 
         def vshare(k):
-            return (CH[k][1] * 5 // 8) // 8 * 2
+            return (CH[k][1] * 9 // 16) // 8 * 2
 
         def regroup_v(k):
             dst = grouped[k][:].rearrange("p (c i) t -> p c t i", i=4)
@@ -139,12 +132,7 @@ def tile_cos_attn_kernel(tc, x, out):
                     in_=rn[:, t:t + 1].to_broadcast([P, P]),
                     identity=ident[:],
                 )
-
-        def copy_s(k):
-            nc.scalar.copy(out=rnj[:, kcols(k)], in_=bb[k][:, 0:CH[k][1]])
-
-        def copy_v(k):
-            nc.vector.tensor_copy(out=rnj[:, kcols(k)], in_=bb[k][:, 0:CH[k][1]])
+            nc.scalar.copy(out=rnj[:, kcols(k)], in_=bc[:, 0:CH[k][1]])
 
         def quant(k):
             nc.vector.quantize_mx(
@@ -152,14 +140,6 @@ def tile_cos_attn_kernel(tc, x, out):
                 scales=scl[:, kcols(k)],
                 in_=grouped[k][:].rearrange("p w t -> p (w t)"),
             )
-
-        def etile(i):
-            if i not in ee:
-                if i < NSRC:
-                    ee[i] = keep[i]
-                else:
-                    ee[i] = rows.tile([P, N], F32, name="row")
-            return ee[i]
 
         def mx(i, c):
             ms = slice(i * P, (i + 1) * P)
@@ -173,72 +153,43 @@ def tile_cos_attn_kernel(tc, x, out):
             )
 
         def scale(i, c):
+            if c == 0:
+                rr[i] = rows.tile([P, N], F32, name="row")
             nc.vector.scalar_tensor_tensor(
-                out=etile(i)[:, cols(c)], in0=pp[(i, c)][:], scalar=rn[:, i:i + 1], in1=rnj[:, cols(c)],
+                out=rr[i][:, cols(c)], in0=pp[(i, c)][:], scalar=rn[:, i:i + 1], in1=rnj[:, cols(c)],
                 op0=ALU.mult, op1=ALU.mult,
             )
 
-        def expo(i, sl, slot):
-            e = etile(i)
+        def expo(i):
+            bias = -1.0
             nc.scalar.activation(
-                out=e[:, sl], in_=e[:, sl], func=ACT.Exp, bias=-1.0, scale=1.0,
-                accum_out=sall[:, i, slot:slot + 1],
+                out=rr[i][:], in_=rr[i][:], func=ACT.Exp, bias=bias, scale=1.0,
+                accum_out=ssum[:, i:i + 1],
             )
 
-        def mirror(i, c):
-            for on_v, a, b in pieces(i, c):
-                t = psum.tile([P, CHUNK], F32, name="tr", tag="b")
-                tt[(i, c, on_v)] = t
-                for blk in range(a // P, b // P):
-                    nc.tensor.transpose(
-                        out=t[:, blk * P:(blk + 1) * P],
-                        in_=keep[c * BPC + blk][:, i * P:(i + 1) * P],
-                        identity=ident[:],
-                    )
+        def norm_g(row, r1, sl):
+            nc.gpsimd.tensor_scalar(out=row[:, sl], in0=row[:, sl], scalar1=r1, scalar2=1.0, op0=ALU.mult, op1=ALU.mult)
 
-        def pieces(i, c):
-            if MIR[i] == 1:
-                if i % 2 == 0:
-                    return [(False, 0, CHUNK)]
-                return [(True, 0, CHUNK // 2), (False, CHUNK // 2, CHUNK)]
-            return [(c == 0, 0, CHUNK)]
+        def norm_v(row, r1, sl):
+            nc.vector.tensor_scalar(out=row[:, sl], in0=row[:, sl], scalar1=r1, scalar2=None, op0=ALU.mult)
 
-        def leave(i, c, vector):
-            e = etile(i)
-            for on_v, a, b in pieces(i, c):
-                if on_v != vector:
-                    continue
-                dst = e[:, c * CHUNK + a:c * CHUNK + b]
-                if on_v:
-                    nc.vector.tensor_scalar(
-                        out=dst, in0=tt[(i, c, on_v)][:, a:b], scalar1=1.0, scalar2=None,
-                        op0=ALU.mult, op1=ALU.add, accum_out=sall[:, i, 8 + c:9 + c],
-                    )
-                else:
-                    nc.scalar.activation(
-                        out=dst, in_=tt[(i, c, on_v)][:, a:b], func=ACT.Copy,
-                        accum_out=sall[:, i, 4 + c:5 + c],
-                    )
+        def norm_s(row, r1, sl):
+            nc.scalar.activation(out=row[:, sl], in_=row[:, sl], func=ACT.Copy, scale=r1)
 
         def finish(i):
             r1 = rs[:, i:i + 1]
-            e = etile(i)
-            if 0 < i and MIR[i] == 0:
-                nc.vector.reciprocal(out=r1, in_=sall[:, i, 0:1])
+            row = rr[i]
+            nc.vector.reciprocal(out=r1, in_=ssum[:, i:i + 1])
+            if i < NT - 2:
+                parts = [(norm_g, slice(0, N))]
+            elif i == NT - 2:
+                parts = [(norm_v, slice(0, 1024)), (norm_v, slice(1024, N))]
             else:
-                nc.vector.tensor_reduce(out=stot[:, i:i + 1], in_=sall[:, i, :], axis=AX.X, op=ALU.add)
-                nc.vector.reciprocal(out=r1, in_=stot[:, i:i + 1])
-            if i < NSRC:
-                o = rows.tile([P, N], F32, name="row")
-            else:
-                o = e
-            vcols = (0, 512 * (1 - i % 2), 256)[MIR[i]]
-            nc.gpsimd.tensor_scalar(
-                out=o[:, vcols:], in0=e[:, vcols:], scalar1=r1, scalar2=1.0, op0=ALU.mult, op1=ALU.mult,
-            )
-            if vcols:
-                nc.vector.tensor_scalar(out=o[:, :vcols], in0=e[:, :vcols], scalar1=r1, scalar2=None, op0=ALU.mult)
-            nc.sync.dma_start(out=ov[i], in_=o[:])
+                parts = [(norm_g, slice(1536, N)), (norm_s, slice(1024, 1536)), (norm_v, slice(0, 1024))]
+            for fn, sl in parts:
+                fn(row, r1, sl)
+            for fn, sl in parts:
+                nc.sync.dma_start(out=ov[i][:, sl], in_=row[:, sl])
 
         last = NK - 1
         for k in range(last):
@@ -247,7 +198,6 @@ def tile_cos_attn_kernel(tc, x, out):
             gram(k)
             if k >= 3:
                 spread(k - 3)
-                copy_s(k - 3)
             if k >= 1:
                 n2mm(k - 1)
                 rsq(k - 1)
@@ -256,17 +206,14 @@ def tile_cos_attn_kernel(tc, x, out):
         gram(last)
         regroup_s(last)
         spread(last - 3)
-        copy_s(last - 3)
         n2mm(last - 1)
         rsq(last - 1)
         mask(last)
         spread(last - 2)
-        copy_s(last - 2)
         n2mm(last)
         rsq(last)
         regroup_v(last)
         spread(last - 1)
-        copy_s(last - 1)
         quant(last - 1)
         quant(last)
         mx(0, 0)
@@ -276,33 +223,13 @@ def tile_cos_attn_kernel(tc, x, out):
         nc.scalar.activation(out=warm[:, 1:2], in_=ones[:, 0:1], func=ACT.Exp)
         mx(0, 3)
 
-        for k in range(NT + 3):
-            if k + 1 < NT:
-                for c in range(MIR[k + 1], NCH):
-                    mx(k + 1, c)
-            if k < NT:
-                for c in range(MIR[k]):
-                    mirror(k, c)
-            direct = list(range(MIR[k], NCH)) if k < NT else [NCH]
-            for c in direct:
-                if k < NT:
-                    if k == 0 and c == 3:
-                        copy_v(last)
-                    scale(k, c)
-                    if k == 0:
-                        expo(0, cols(c), c)
-                if c == direct[0]:
-                    if 1 <= k <= NT:
-                        for c2 in range(MIR[k - 1]):
-                            leave(k - 1, c2, True)
-                    if 4 <= k and k - 2 < NT:
-                        finish(k - 2)
-                if k == 1 and c == 1:
-                    finish(0)
-                if k == 2 and c == 2:
-                    finish(1)
-            if 0 < k < NT:
-                expo(k, slice(MIR[k] * CHUNK, N), 0)
-            if k < NT:
-                for c2 in range(MIR[k]):
-                    leave(k, c2, False)
+        for i in range(NT + 2):
+            for c in range(NCH):
+                if i < NT:
+                    if i > 0:
+                        mx(i, c)
+                    scale(i, c)
+                if c == 0 and i >= 2:
+                    finish(i - 2)
+            if i < NT:
+                expo(i)

@@ -61,6 +61,7 @@ def tile_cos_attn_kernel(tc, x, out):
         rn = const.tile([P, NT], F32, name="rn")
         ssum = const.tile([P, NT], F32, name="ssum")
         rs = const.tile([P, NT], F32, name="rs")
+        nmx = const.tile([P, NT], F32, name="nmx")
         grouped = [const.tile([P, CH[k][1], PACK], BF16, name="grouped%d" % k, align_bytes=64) for k in range(NK)]
         dd = [const.tile([P, CH[k][1]], F32, name="dd%d" % k) for k in range(NK)]
         n2 = psum.tile([P, CHUNK], F32, name="n2", tag="b")
@@ -161,7 +162,7 @@ def tile_cos_attn_kernel(tc, x, out):
             )
 
         def expo(i):
-            bias = -1.0
+            bias = nmx[:, i:i + 1]
             nc.scalar.activation(
                 out=rr[i][:], in_=rr[i][:], func=ACT.Exp, bias=bias, scale=1.0,
                 accum_out=ssum[:, i:i + 1],
@@ -180,15 +181,12 @@ def tile_cos_attn_kernel(tc, x, out):
             r1 = rs[:, i:i + 1]
             row = rr[i]
             nc.vector.reciprocal(out=r1, in_=ssum[:, i:i + 1])
-            if i < NT - 2:
+            if i < NT - 1:
                 parts = [(norm_g, slice(0, N))]
-            elif i == NT - 2:
-                parts = [(norm_v, slice(0, 1024)), (norm_v, slice(1024, N))]
             else:
-                parts = [(norm_g, slice(1536, N)), (norm_s, slice(1024, 1536)), (norm_v, slice(0, 1024))]
+                parts = [(norm_v, slice(0, 1024)), (norm_s, slice(1024, 1536)), (norm_g, slice(1536, N))]
             for fn, sl in parts:
                 fn(row, r1, sl)
-            for fn, sl in parts:
                 nc.sync.dma_start(out=ov[i][:, sl], in_=row[:, sl])
 
         last = NK - 1
@@ -223,13 +221,14 @@ def tile_cos_attn_kernel(tc, x, out):
         nc.scalar.activation(out=warm[:, 1:2], in_=ones[:, 0:1], func=ACT.Exp)
         mx(0, 3)
 
-        for i in range(NT + 2):
-            for c in range(NCH):
-                if i < NT:
+        for i in range(NT + 1):
+            if i < NT:
+                for c in range(NCH):
                     if i > 0:
                         mx(i, c)
                     scale(i, c)
-                if c == 0 and i >= 2:
-                    finish(i - 2)
+                nc.vector.tensor_reduce(out=nmx[:, i:i + 1], in_=rr[i][:], axis=AX.X, op=ALU.max, negate=True)
+            if i >= 1:
+                finish(i - 1)
             if i < NT:
                 expo(i)

@@ -61,7 +61,6 @@ def tile_cos_attn_kernel(tc, x, out):
         rn = const.tile([P, NT], F32, name="rn")
         ssum = const.tile([P, NT], F32, name="ssum")
         rs = const.tile([P, NT], F32, name="rs")
-        nmx = const.tile([P, NT], F32, name="nmx")
         grouped = [const.tile([P, CH[k][1], PACK], BF16, name="grouped%d" % k, align_bytes=64) for k in range(NK)]
         dd = [const.tile([P, CH[k][1]], F32, name="dd%d" % k) for k in range(NK)]
         n2 = psum.tile([P, CHUNK], F32, name="n2", tag="b")
@@ -156,15 +155,11 @@ def tile_cos_attn_kernel(tc, x, out):
         def scale(i, c):
             if c == 0:
                 rr[i] = rows.tile([P, N], F32, name="row")
-            nc.vector.scalar_tensor_tensor(
-                out=rr[i][:, cols(c)], in0=pp[(i, c)][:], scalar=rn[:, i:i + 1], in1=rnj[:, cols(c)],
-                op0=ALU.mult, op1=ALU.mult,
-            )
+            nc.vector.tensor_tensor(out=rr[i][:, cols(c)], in0=pp[(i, c)][:], in1=rnj[:, cols(c)], op=ALU.mult)
 
         def expo(i):
-            bias = nmx[:, i:i + 1]
             nc.scalar.activation(
-                out=rr[i][:], in_=rr[i][:], func=ACT.Exp, bias=bias, scale=1.0,
+                out=rr[i][:], in_=rr[i][:], func=ACT.Exp, bias=-1.0, scale=rn[:, i:i + 1],
                 accum_out=ssum[:, i:i + 1],
             )
 
@@ -181,12 +176,15 @@ def tile_cos_attn_kernel(tc, x, out):
             r1 = rs[:, i:i + 1]
             row = rr[i]
             nc.vector.reciprocal(out=r1, in_=ssum[:, i:i + 1])
-            if i < NT - 1:
+            if i < NT - 2:
                 parts = [(norm_g, slice(0, N))]
+            elif i == NT - 2:
+                parts = [(norm_v, slice(0, 1024)), (norm_v, slice(1024, N))]
             else:
-                parts = [(norm_v, slice(0, 1024)), (norm_s, slice(1024, 1536)), (norm_g, slice(1536, N))]
+                parts = [(norm_g, slice(1536, N)), (norm_s, slice(1024, 1536)), (norm_v, slice(0, 1024))]
             for fn, sl in parts:
                 fn(row, r1, sl)
+            for fn, sl in parts:
                 nc.sync.dma_start(out=ov[i][:, sl], in_=row[:, sl])
 
         last = NK - 1
@@ -221,14 +219,13 @@ def tile_cos_attn_kernel(tc, x, out):
         nc.scalar.activation(out=warm[:, 1:2], in_=ones[:, 0:1], func=ACT.Exp)
         mx(0, 3)
 
-        for i in range(NT + 1):
-            if i < NT:
-                for c in range(NCH):
+        for i in range(NT + 2):
+            for c in range(NCH):
+                if i < NT:
                     if i > 0:
                         mx(i, c)
                     scale(i, c)
-                nc.vector.tensor_reduce(out=nmx[:, i:i + 1], in_=rr[i][:], axis=AX.X, op=ALU.max, negate=True)
-            if i >= 1:
-                finish(i - 1)
+                if c == 0 and i >= 2:
+                    finish(i - 2)
             if i < NT:
                 expo(i)

@@ -63,7 +63,6 @@ def tile_cos_attn_kernel(tc, x, out):
         rs = const.tile([P, NT], F32, name="rs")
         grouped = [const.tile([P, CH[k][1], PACK], BF16, name="grouped%d" % k, align_bytes=64) for k in range(NK)]
         dd = [const.tile([P, CH[k][1]], F32, name="dd%d" % k) for k in range(NK)]
-        n2 = psum.tile([P, CHUNK], F32, name="n2", tag="b")
         gg = {}
         bb = {}
         pp = {}
@@ -111,35 +110,29 @@ def tile_cos_attn_kernel(tc, x, out):
                 op=ALU.mult,
             )
 
-        def n2mm(k):
-            for b in range(CH[k][1] // P):
-                t = CH[k][0] // P + b
-                nc.tensor.matmul(
-                    out=n2[:, t:t + 1], lhsT=dd[k][:, b * P:(b + 1) * P], rhs=ones[:, 0:1],
-                    start=True, stop=True,
-                )
-
-        def rsq(k):
-            nc.scalar.activation(out=rn[:, tcols(k)], in_=n2[:, tcols(k)], func=ACT.Abs_reciprocal_sqrt)
-
-        def spread(k):
-            bc = psum.tile([P, CHUNK], F32, name="bc", tag="b")
-            bb[k] = bc
-            for b in range(CH[k][1] // P):
-                t = CH[k][0] // P + b
-                nc.tensor.transpose(
-                    out=bc[:, b * P:(b + 1) * P],
-                    in_=rn[:, t:t + 1].to_broadcast([P, P]),
-                    identity=ident[:],
-                )
-            nc.scalar.copy(out=rnj[:, kcols(k)], in_=bc[:, 0:CH[k][1]])
-
         def quant(k):
             nc.vector.quantize_mx(
                 out=codes[:, kcols(k)].bitcast(FP8X4),
                 scales=scl[:, kcols(k)],
                 in_=grouped[k][:].rearrange("p w t -> p (w t)"),
             )
+
+        ones_sq = const.tile([P, P], F32, name="ones_sq")
+        nc.gpsimd.memset(ones_sq[:], 1.0)
+
+        def bcast(k):
+            bc = psum.tile([P, CHUNK], F32, name="bc", tag="b")
+            nc.tensor.matmul(out=bc[:, 0:CH[k][1]], lhsT=ones_sq[:], rhs=dd[k][:], start=True, stop=True)
+            nc.scalar.activation(out=rnj[:, kcols(k)], in_=bc[:, 0:CH[k][1]], func=ACT.Abs_reciprocal_sqrt)
+
+        def rnpart(k):
+            tp = psum.tile([P, CHUNK], F32, name="tp", tag="b")
+            nb = CH[k][1] // P
+            for b in range(nb):
+                nc.tensor.transpose(
+                    out=tp[:, b * P:(b + 1) * P], in_=rnj[:, CH[k][0] + b * P:CH[k][0] + (b + 1) * P], identity=ident[:],
+                )
+            nc.scalar.copy(out=rn[:, tcols(k)], in_=tp[:, 0:CH[k][1]].rearrange("p (b n) -> p b n", b=nb)[:, :, 0])
 
         def mx(i, c):
             ms = slice(i * P, (i + 1) * P)
@@ -188,36 +181,27 @@ def tile_cos_attn_kernel(tc, x, out):
                 nc.sync.dma_start(out=ov[i][:, sl], in_=row[:, sl])
 
         last = NK - 1
-        for k in range(last):
+        for k in range(NK):
             regroup_v(k)
             regroup_s(k)
             gram(k)
-            if k >= 3:
-                spread(k - 3)
             if k >= 1:
-                n2mm(k - 1)
-                rsq(k - 1)
+                bcast(k - 1)
                 quant(k - 1)
+            if k == 2:
+                rnpart(0)
+            if k == 3:
+                rnpart(1)
             mask(k)
-        gram(last)
-        regroup_s(last)
-        spread(last - 3)
-        n2mm(last - 1)
-        rsq(last - 1)
-        mask(last)
-        spread(last - 2)
-        n2mm(last)
-        rsq(last)
-        regroup_v(last)
-        spread(last - 1)
-        quant(last - 1)
+        bcast(last)
+        nc.scalar.activation(out=warm[:, 1:2], in_=ones[:, 0:1], func=ACT.Exp)
         quant(last)
         mx(0, 0)
         mx(0, 1)
         mx(0, 2)
-        spread(last)
-        nc.scalar.activation(out=warm[:, 1:2], in_=ones[:, 0:1], func=ACT.Exp)
         mx(0, 3)
+        for k in range(2, NK):
+            rnpart(k)
 
         for i in range(NT + 2):
             for c in range(NCH):

from contextlib import ExitStack

import concourse.mybir as mybir
from concourse.masks import make_identity

F32 = mybir.dt.float32
BF16 = mybir.dt.bfloat16
U32 = mybir.dt.uint32
U8 = mybir.dt.uint8
FP8X4 = mybir.dt.float8_e4m3fn_x4
ACT = mybir.ActivationFunctionType
ALU = mybir.AluOpType
AX = mybir.AxisListType

P = 128
C = 512
N = 2048
PACK = 4
CHUNK = 512
NCH = N // CHUNK
NT = N // P
BPC = CHUNK // P
FLOPS = 2 * N * N * C
CH = [(0,256),(256,256),(512,512),(1024,512),(1536,512)]
NK = len(CH)
NWARM = 4


def tile_cos_attn_kernel(tc, x, out):
    nc = tc.nc
    xv = x.rearrange("(p j) w h -> p j (w h)", j=PACK)
    ov = out.rearrange("o (t p) n -> (o t) p n", p=P)
    with ExitStack() as ctx:
        ctx.enter_context(tc.manual_schedule())
        const = ctx.enter_context(tc.tile_pool(name="const", bufs=1))
        rows = ctx.enter_context(tc.tile_pool(name="rows", bufs=8))
        psum = ctx.enter_context(tc.psum_pool(name="psum", bufs=8))

        raw = []
        for k in range(NK):
            st, sz = CH[k]
            r = const.tile([P, PACK, sz], BF16, name="raw%d" % k)
            nc.sync.dma_start(out=r[:], in_=xv[:, :, st:st + sz])
            raw.append(r)

        wz = const.tile([P, CHUNK], BF16, name="wz")
        nc.vector.memset(wz[:], 0.0)
        wp = psum.tile([P, CHUNK], F32, name="wp", tag="b")
        for w in range(NWARM):
            nc.tensor.matmul(out=wp[:], lhsT=wz[:, 0:P], rhs=wz[:], start=True, stop=True)
        ident = const.tile([P, P], F32, name="ident")
        make_identity(nc, ident[:])
        ones = const.tile([P, 2], F32, name="ones")
        nc.vector.memset(ones[:], 1.0)
        warm = const.tile([P, 2], F32, name="warm")
        nc.scalar.activation(out=warm[:, 0:1], in_=ones[:, 0:1], func=ACT.Abs_reciprocal_sqrt)

        codes = const.tile([P, N], U32, name="codes", align_bytes=64)
        scl = const.tile([P, N], U8, name="scl", align_bytes=64)
        rnj = const.tile([P, N], F32, name="rnj")
        rn = const.tile([P, NT], F32, name="rn")
        ssum = const.tile([P, NT], F32, name="ssum")
        rs = const.tile([P, NT], F32, name="rs")
        grouped = [const.tile([P, CH[k][1], PACK], BF16, name="grouped%d" % k, align_bytes=64) for k in range(NK)]
        dd = [const.tile([P, CH[k][1]], F32, name="dd%d" % k) for k in range(NK)]
        gg = {}
        bb = {}
        pp = {}
        rr = {}

        def cols(c):
            return slice(c * CHUNK, (c + 1) * CHUNK)

        def kcols(k):
            return slice(CH[k][0], CH[k][0] + CH[k][1])

        def tcols(k):
            return slice(CH[k][0] // P, (CH[k][0] + CH[k][1]) // P)

        def vshare(k):
            return (CH[k][1] * 9 // 16) // 8 * 2

        def regroup_v(k):
            dst = grouped[k][:].rearrange("p (c i) t -> p c t i", i=4)
            src = raw[k][:].rearrange("p t (c i) -> p c t i", i=4)
            nc.vector.tensor_copy(out=dst[:, :vshare(k)], in_=src[:, :vshare(k)])

        def regroup_s(k):
            dst = grouped[k][:].rearrange("p (c i) t -> p c t i", i=4)
            src = raw[k][:].rearrange("p t (c i) -> p c t i", i=4)
            nc.scalar.copy(out=dst[:, vshare(k):], in_=src[:, vshare(k):])

        def gram(k):
            g = psum.tile([P, CHUNK], F32, name="g", tag="b")
            gg[k] = g
            for b in range(CH[k][1] // P):
                bs = slice(b * P, (b + 1) * P)
                for j in range(PACK):
                    nc.tensor.matmul(
                        out=g[:, bs], lhsT=raw[k][:, j, bs], rhs=raw[k][:, j, bs],
                        start=(j == 0), stop=(j == PACK - 1),
                    )

        def mask(k):
            nb = CH[k][1] // P
            nc.vector.tensor_tensor(
                out=dd[k][:].rearrange("p (b n) -> p b n", b=nb),
                in0=gg[k][:, 0:CH[k][1]].rearrange("p (b n) -> p b n", b=nb),
                in1=ident[:].unsqueeze(1).to_broadcast([P, nb, P]),
                op=ALU.mult,
            )

        def quant(k):
            nc.vector.quantize_mx(
                out=codes[:, kcols(k)].bitcast(FP8X4),
                scales=scl[:, kcols(k)],
                in_=grouped[k][:].rearrange("p w t -> p (w t)"),
            )

        ones_sq = const.tile([P, P], F32, name="ones_sq")
        nc.gpsimd.memset(ones_sq[:], 1.0)

        def bcast(k):
            bc = psum.tile([P, CHUNK], F32, name="bc", tag="b")
            nc.tensor.matmul(out=bc[:, 0:CH[k][1]], lhsT=ones_sq[:], rhs=dd[k][:], start=True, stop=True)
            nc.scalar.activation(out=rnj[:, kcols(k)], in_=bc[:, 0:CH[k][1]], func=ACT.Abs_reciprocal_sqrt)

        def rnpart(k):
            tp = psum.tile([P, CHUNK], F32, name="tp", tag="b")
            nb = CH[k][1] // P
            for b in range(nb):
                nc.tensor.transpose(
                    out=tp[:, b * P:(b + 1) * P], in_=rnj[:, CH[k][0] + b * P:CH[k][0] + (b + 1) * P], identity=ident[:],
                )
            nc.scalar.copy(out=rn[:, tcols(k)], in_=tp[:, 0:CH[k][1]].rearrange("p (b n) -> p b n", b=nb)[:, :, 0])

        def mx(i, c):
            ms = slice(i * P, (i + 1) * P)
            ps = psum.tile([P, CHUNK], F32, name="ps", tag="b")
            pp[(i, c)] = ps
            nc.tensor.matmul_mx(
                out=ps[:],
                lhsT=codes[:, ms].bitcast(FP8X4), lhsT_scale=scl[:, ms],
                rhs=codes[:, cols(c)].bitcast(FP8X4), rhs_scale=scl[:, cols(c)],
                start=True, stop=True,
            )

        def scale(i, c):
            if c == 0:
                rr[i] = rows.tile([P, N], F32, name="row")
            nc.vector.tensor_tensor(out=rr[i][:, cols(c)], in0=pp[(i, c)][:], in1=rnj[:, cols(c)], op=ALU.mult)

        def expo(i):
            nc.scalar.activation(
                out=rr[i][:], in_=rr[i][:], func=ACT.Exp, bias=-1.0, scale=rn[:, i:i + 1],
                accum_out=ssum[:, i:i + 1],
            )

        def norm_g(row, r1, sl):
            nc.gpsimd.tensor_scalar(out=row[:, sl], in0=row[:, sl], scalar1=r1, scalar2=1.0, op0=ALU.mult, op1=ALU.mult)

        def norm_v(row, r1, sl):
            nc.vector.tensor_scalar(out=row[:, sl], in0=row[:, sl], scalar1=r1, scalar2=None, op0=ALU.mult)

        def norm_s(row, r1, sl):
            nc.scalar.activation(out=row[:, sl], in_=row[:, sl], func=ACT.Copy, scale=r1)

        def finish(i):
            r1 = rs[:, i:i + 1]
            row = rr[i]
            nc.vector.reciprocal(out=r1, in_=ssum[:, i:i + 1])
            if i < NT - 2:
                parts = [(norm_g, slice(0, N))]
            elif i == NT - 2:
                parts = [(norm_v, slice(0, 1024)), (norm_v, slice(1024, N))]
            else:
                parts = [(norm_g, slice(1536, N)), (norm_s, slice(1024, 1536)), (norm_v, slice(0, 1024))]
            for fn, sl in parts:
                fn(row, r1, sl)
            for fn, sl in parts:
                nc.sync.dma_start(out=ov[i][:, sl], in_=row[:, sl])

        last = NK - 1
        for k in range(NK):
            regroup_v(k)
            regroup_s(k)
            gram(k)
            if k >= 1:
                bcast(k - 1)
                quant(k - 1)
            if k == 2:
                rnpart(0)
            if k == 3:
                rnpart(1)
            mask(k)
        bcast(last)
        nc.scalar.activation(out=warm[:, 1:2], in_=ones[:, 0:1], func=ACT.Exp)
        quant(last)
        mx(0, 0)
        mx(0, 1)
        mx(0, 2)
        mx(0, 3)
        for k in range(2, NK):
            rnpart(k)

        for i in range(NT + 2):
            for c in range(NCH):
                if i < NT:
                    if i > 0:
                        mx(i, c)
                    scale(i, c)
                if c == 0 and i >= 2:
                    finish(i - 2)
            if i < NT:
                expo(i)
